import numpy as np
import ml_dtypes


BF16 = ml_dtypes.bfloat16


def bf(x):
    return np.asarray(x, np.float32).astype(BF16)


def f64(x):
    return np.asarray(x).astype(np.float64)


E2M1 = np.array([0.0, 0.5, 1.0, 1.5, 2.0, 3.0, 4.0, 6.0, -0.0, -0.5, -1.0, -1.5, -2.0, -3.0, -4.0, -6.0])


def pack_weight(w, fmt):
    k, n = w.shape
    w = f64(bf(w)).reshape(k // 32, 32, n)
    amax = np.abs(w).max(1)
    if fmt == "e4m3":
        byte = np.frexp(amax)[1] - 1 + 127 - 7
    else:
        mant, ex = np.frexp(amax / 6.0)
        byte = np.where(mant > 0.5, ex, ex - 1) + 127
    byte = np.clip(np.where(amax > 0, byte, 1), 1, 254)
    scaled = (w * np.exp2(127.0 - byte)[:, None, :]).reshape(k, n).astype(np.float32)
    by_word = np.ascontiguousarray(scaled.reshape(k // 512, 128, 4, n).transpose(0, 1, 3, 2))
    if fmt == "e4m3":
        words = by_word.astype(ml_dtypes.float8_e4m3fn).view(np.uint8)
    else:
        c = by_word.astype(ml_dtypes.float4_e2m1fn).view(np.uint8) & 0xF
        words = c[..., 0::2] | (c[..., 1::2] << 4)
    return np.ascontiguousarray(words), np.ascontiguousarray(byte.astype(np.uint8).reshape(k // 512, 16, n))


def unpack_weight(words, scales, fmt):
    g, p, n, _ = words.shape
    if fmt == "e4m3":
        vals = np.ascontiguousarray(words).view(ml_dtypes.float8_e4m3fn).astype(np.float64)
    else:
        nib = np.empty((g, p, n, 4), np.uint8)
        nib[..., 0::2] = words & 0xF
        nib[..., 1::2] = words >> 4
        vals = E2M1[nib]
    vals = vals * np.repeat(np.exp2(scales.astype(np.float64) - 127.0), 8, axis=1)[..., None]
    return vals.transpose(0, 1, 3, 2).reshape(g * 512, n)

def pack4(w):
    words, scales = pack_weight(w, "e2m1")
    return words.reshape(words.shape[0], 128, -1), scales


def unpack4(words, scales):
    return unpack_weight(words.reshape(words.shape[0], 128, -1, 2), scales, "e2m1")


def kspread(k):
    return np.exp2(np.repeat(np.random.randint(-6, 7, k // 32), 32).astype(np.float64))


B, S, D = 5, 512, 2048
ROPE_BASE = 10000.0


def rope_tables():
    inv_freq = 1.0 / ROPE_BASE ** (np.arange(0, D, 2) / D)
    freqs = np.outer(np.arange(S), inv_freq)
    emb = np.concatenate([freqs, freqs], axis=-1)
    return np.cos(emb), np.sin(emb)


def rotate_half(u):
    u1, u2 = np.split(u, 2, axis=-1)
    return np.concatenate([-u2, u1], axis=-1)


def setup_inputs():
    s = kspread(D)
    c, sn = rope_tables()
    w = 1.0 / np.sqrt(D)
    x = np.random.standard_normal((B, S, D)) * s
    wq = np.random.standard_normal((D, D)) * w / s[None, :]
    wk = np.random.standard_normal((D, D)) * w / s[None, :]
    x_words, x_scales = pack4(np.ascontiguousarray(x.reshape(B * S, D).T))
    wq_words, wq_scales = pack4(np.ascontiguousarray(wq.T))
    wk_words, wk_scales = pack4(np.ascontiguousarray(wk.T))
    return {"x_words": x_words,
            "x_scales": x_scales,
            "cos": bf(c),
            "sin": bf(sn),
            "Wq_words": wq_words,
            "Wq_scales": wq_scales,
            "Wk_words": wk_words,
            "Wk_scales": wk_scales}


def reference(x_words, x_scales, cos, sin, Wq_words, Wq_scales, Wk_words, Wk_scales):
    xq = unpack4(x_words, x_scales).T.reshape(B, S, D)
    q = xq @ unpack4(Wq_words, Wq_scales)
    k = xq @ unpack4(Wk_words, Wk_scales)
    c, sn = f64(cos), f64(sin)
    q_rot = q * c + rotate_half(q) * sn
    k_rot = k * c + rotate_half(k) * sn
    return q_rot, k_rot

@@ -1,0 +1,182 @@
+from contextlib import ExitStack
+
+import concourse.mybir as mybir
+
+F32 = mybir.dt.float32
+BF16 = mybir.dt.bfloat16
+I32 = mybir.dt.int32
+U8 = mybir.dt.uint8
+FP4X4 = mybir.dt.float4_e2m1fn_x4
+MULT = mybir.AluOpType.mult
+ADD = mybir.AluOpType.add
+
+B, S, D = 5, 512, 2048
+P = 128
+PASSES = D // 512
+NB = 512
+
+FLOPS = 2 * B * S * D * 2 * D
+
+
+def tile_attention_pa_kernel(
+    tc, x_words, x_scales, cos, sin, Wq_words, Wq_scales, Wk_words, Wk_scales, out_0, out_1
+):
+    nc = tc.nc
+    w_words = (Wq_words, Wk_words)
+    w_scales = (Wq_scales, Wk_scales)
+    outs = (out_0, out_1)
+
+    cos_v = cos.rearrange("(t p) (n c) -> t p n c", p=P, c=NB)
+    sin_v = sin.rearrange("(t p) (n c) -> t p n c", p=P, c=NB)
+    out_v = [o.rearrange("b (t p) (n c) -> b t p n c", p=P, c=NB) for o in outs]
+    x_v = x_words.rearrange("g p c -> p g c")
+    w_v = [w.rearrange("g p c -> p g c") for w in w_words]
+
+    with ExitStack() as ctx:
+        ctx.enter_context(tc.manual_schedule())
+        keep = ctx.enter_context(tc.tile_pool(name="keep", bufs=1))
+        work = ctx.enter_context(tc.tile_pool(name="work", bufs=5))
+        psum = ctx.enter_context(tc.psum_pool(name="psum", bufs=8))
+
+        xc = {}
+        for b in range(B):
+            for pp in range(2):
+                xc[(b, pp)] = keep.tile([P, PASSES, 512], U8, name="xc%d_%d" % (b, pp), align_bytes=64)
+        xs = [keep.tile([P, PASSES, S], U8, name="xs%d" % b, align_bytes=64) for b in range(B)]
+        wc = {}
+        for proj in range(2):
+            for n in range(4):
+                wc[(proj, n)] = keep.tile([P, PASSES, 2 * NB], U8, name="wc%d_%d" % (proj, n), align_bytes=64)
+        wsq = [keep.tile([P, PASSES, NB], U8, name="wsq%d" % n, align_bytes=64) for n in range(4)]
+        wsk = keep.tile([P, PASSES, D], U8, name="wsk", align_bytes=64)
+        th = {}
+        for pt in range(4):
+            for h in range(2):
+                th[(pt, h)] = keep.tile([P, 4, NB], BF16, name="th%d_%d" % (pt, h))
+
+        def load_table(eng, pt, h):
+            eng.dma_start(out=th[(pt, h)][:, 0:2, :], in_=cos_v[pt, :, h:4:2, :])
+            eng.dma_start(out=th[(pt, h)][:, 2:4, :], in_=sin_v[pt, :, h:4:2, :])
+
+        def negate_table(pt, h):
+            nc.scalar.mul(out=th[(pt, h)][:, 2, :], in_=th[(pt, h)][:, 2, :], mul=-1.0)
+
+        def load_scales(plane, src, c0, ncols):
+            for q in range(4):
+                nc.sync.dma_start(
+                    out=plane[32 * q : 32 * q + 4, :, :].bitcast(I32),
+                    in_=src[:, 4 * q : 4 * q + 4, c0 : c0 + ncols].rearrange("g r n -> r g n").bitcast(I32),
+                )
+
+        def load_x_codes(b, pp):
+            off = 2 * (S * b + 256 * pp)
+            nc.sync.dma_start(out=xc[(b, pp)][:].bitcast(I32), in_=x_v[:, :, off : off + 512].bitcast(I32))
+
+        def load_w_codes(proj, n):
+            nc.sync.dma_start(
+                out=wc[(proj, n)][:].bitcast(I32),
+                in_=w_v[proj][:, :, 2 * NB * n : 2 * NB * (n + 1)].bitcast(I32),
+            )
+
+        load_table(nc.gpsimd, 0, 0)
+        load_table(nc.gpsimd, 1, 0)
+        for plane in (xs[0], wsq[0], wsq[2], xs[1]):
+            nc.vector.memset(plane[:].bitcast(I32), 0)
+        for plane in (xs[2], xs[3], xs[4], wsk, wsq[1], wsq[3]):
+            nc.gpsimd.memset(plane[:].bitcast(F32), 0.0)
+
+        load_w_codes(0, 0)
+        load_x_codes(0, 0)
+        load_scales(xs[0], x_scales, 0, S)
+        load_scales(wsq[0], Wq_scales, 0, NB)
+        load_w_codes(0, 2)
+        load_scales(wsq[2], Wq_scales, 2 * NB, NB)
+        for b in range(1, B):
+            load_scales(xs[b], x_scales, S * b, S)
+            load_x_codes(b, 0)
+        load_x_codes(0, 1)
+        load_table(nc.sync, 2, 0)
+        load_table(nc.sync, 3, 0)
+        for b in range(1, B):
+            load_x_codes(b, 1)
+        load_w_codes(1, 0)
+        load_w_codes(1, 2)
+        load_scales(wsk, Wk_scales, 0, D)
+        load_w_codes(0, 1)
+        load_w_codes(0, 3)
+        load_scales(wsq[1], Wq_scales, NB, NB)
+        load_scales(wsq[3], Wq_scales, 3 * NB, NB)
+        for pt in range(4):
+            load_table(nc.sync, pt, 1)
+        load_w_codes(1, 1)
+        load_w_codes(1, 3)
+
+        for pt in range(4):
+            negate_table(pt, 0)
+
+        def bank(ab, proj, h, pp, b, u, half):
+            n = h + 2 * half
+            acc = psum.tile([P, NB], F32, name="acc")
+            for g in range(PASSES):
+                if proj == 0:
+                    rs = wsq[n][:, g, :]
+                else:
+                    rs = wsk[:, g, NB * n : NB * (n + 1)]
+                nc.tensor.matmul_mx(
+                    out=acc[:],
+                    lhsT=xc[(b, pp)][:, g, 256 * u : 256 * (u + 1)].bitcast(FP4X4),
+                    lhsT_scale=xs[b][:, g, 256 * pp + P * u : 256 * pp + P * (u + 1)],
+                    rhs=wc[(proj, n)][:, g, :].bitcast(FP4X4),
+                    rhs_scale=rs,
+                    start=(g == 0),
+                    stop=(g == PASSES - 1),
+                )
+            table = th[(2 * pp + u, h)]
+            if half == 0:
+                dst = ab[:, 2 * u : 2 * u + 6 : 5, :]
+                tab = table[:, 0:4:3, :]
+            else:
+                dst = ab[:, 2 * u + 1 : 2 * u + 5 : 3, :]
+                tab = table[:, 1:3, :]
+            nc.vector.tensor_tensor(
+                out=dst, in0=acc[:].unsqueeze(1).to_broadcast([P, 2, NB]), in1=tab, op=MULT
+            )
+
+        def store(ab, proj, h, pp, b, u):
+            nc.scalar.dma_start(out=out_v[proj][b, 2 * pp + u, :, h:4:2, :], in_=ab[:, 2 * u : 2 * u + 2, :])
+
+        units = []
+        for proj, h in ((0, 0), (1, 0), (0, 1), (1, 1)):
+            for pp in range(2):
+                for b in range(B):
+                    units.append((proj, h, pp, b))
+
+        for k, (proj, h, pp, b) in enumerate(units):
+            if k == 4:
+                for pt in range(4):
+                    negate_table(pt, 1)
+            ab = work.tile([P, 8, NB], F32, name="ab")
+            if k < len(units) - 2:
+                for half in range(2):
+                    for u in range(2):
+                        bank(ab, proj, h, pp, b, u, half)
+                nc.gpsimd.tensor_tensor(out=ab[:, 0:4, :], in0=ab[:, 0:4, :], in1=ab[:, 4:8, :], op=ADD)
+                for u in range(2):
+                    store(ab, proj, h, pp, b, u)
+            else:
+                for u in range(2):
+                    for half in range(2):
+                        bank(ab, proj, h, pp, b, u, half)
+                    if k == len(units) - 1 and u == 1:
+                        for j in (2, 3):
+                            nc.vector.tensor_tensor(
+                                out=ab[:, j, :], in0=ab[:, j, :], in1=ab[:, j + 4, :], op=ADD
+                            )
+                    else:
+                        nc.gpsimd.tensor_tensor(
+                            out=ab[:, 2 * u : 2 * u + 2, :],
+                            in0=ab[:, 2 * u : 2 * u + 2, :],
+                            in1=ab[:, 2 * u + 4 : 2 * u + 6, :],
+                            op=ADD,
+                        )
+                    store(ab, proj, h, pp, b, u)

@@ -14,8 +14,21 @@ B, S, D = 5, 512, 2048
 P = 128
 PASSES = D // 512
 NB = 512
+U = 4
+V_BLOCKS = 5
+WARM = 12
 
 FLOPS = 2 * B * S * D * 2 * D
+
+
+def add_sizes(j):
+    if j == 0:
+        return (1, 1, 2)
+    if j < 7:
+        return (2, 2)
+    if j < 18:
+        return (4,)
+    return (2, 1, 1)
 
 
 def tile_attention_pa_kernel(
@@ -23,7 +36,6 @@ def tile_attention_pa_kernel(
 ):
     nc = tc.nc
     w_words = (Wq_words, Wk_words)
-    w_scales = (Wq_scales, Wk_scales)
     outs = (out_0, out_1)
 
     cos_v = cos.rearrange("(t p) (n c) -> t p n c", p=P, c=NB)
@@ -35,7 +47,7 @@ def tile_attention_pa_kernel(
     with ExitStack() as ctx:
         ctx.enter_context(tc.manual_schedule())
         keep = ctx.enter_context(tc.tile_pool(name="keep", bufs=1))
-        work = ctx.enter_context(tc.tile_pool(name="work", bufs=5))
+        work = ctx.enter_context(tc.tile_pool(name="work", bufs=3))
         psum = ctx.enter_context(tc.psum_pool(name="psum", bufs=8))
 
         xc = {}
@@ -61,8 +73,8 @@ def tile_attention_pa_kernel(
         def negate_table(pt, h):
             nc.scalar.mul(out=th[(pt, h)][:, 2, :], in_=th[(pt, h)][:, 2, :], mul=-1.0)
 
-        def load_scales(plane, src, c0, ncols):
-            for q in range(4):
+        def load_scales(plane, src, c0, ncols, quads):
+            for q in quads:
                 nc.sync.dma_start(
                     out=plane[32 * q : 32 * q + 4, :, :].bitcast(I32),
                     in_=src[:, 4 * q : 4 * q + 4, c0 : c0 + ncols].rearrange("g r n -> r g n").bitcast(I32),
@@ -78,21 +90,31 @@ def tile_attention_pa_kernel(
                 in_=w_v[proj][:, :, 2 * NB * n : 2 * NB * (n + 1)].bitcast(I32),
             )
 
+        ALL = (0, 1, 2, 3)
+
+        nc.gpsimd.memset(xs[0][:].bitcast(F32), 0.0)
+        if WARM:
+            zero = keep.tile([P, NB], BF16, name="zero")
+            nc.gpsimd.memset(zero[:], 0.0)
+            warm = psum.tile([P, NB], F32, name="acc")
+            for r in range(WARM):
+                nc.tensor.matmul(out=warm[:], lhsT=zero[:, 0:P], rhs=zero[:], start=True, stop=True)
         load_table(nc.gpsimd, 0, 0)
         load_table(nc.gpsimd, 1, 0)
-        for plane in (xs[0], wsq[0], wsq[2], xs[1]):
+        for plane in (wsq[0], wsq[2], xs[1]):
             nc.vector.memset(plane[:].bitcast(I32), 0)
         for plane in (xs[2], xs[3], xs[4], wsk, wsq[1], wsq[3]):
             nc.gpsimd.memset(plane[:].bitcast(F32), 0.0)
 
-        load_w_codes(0, 0)
         load_x_codes(0, 0)
-        load_scales(xs[0], x_scales, 0, S)
-        load_scales(wsq[0], Wq_scales, 0, NB)
+        load_scales(xs[0], x_scales, 0, S, ALL)
+        load_scales(wsq[0], Wq_scales, 0, NB, (0, 1))
+        load_w_codes(0, 0)
+        load_scales(wsq[0], Wq_scales, 0, NB, (2, 3))
         load_w_codes(0, 2)
-        load_scales(wsq[2], Wq_scales, 2 * NB, NB)
+        load_scales(wsq[2], Wq_scales, 2 * NB, NB, ALL)
         for b in range(1, B):
-            load_scales(xs[b], x_scales, S * b, S)
+            load_scales(xs[b], x_scales, S * b, S, ALL)
             load_x_codes(b, 0)
         load_x_codes(0, 1)
         load_table(nc.sync, 2, 0)
@@ -101,11 +123,11 @@ def tile_attention_pa_kernel(
             load_x_codes(b, 1)
         load_w_codes(1, 0)
         load_w_codes(1, 2)
-        load_scales(wsk, Wk_scales, 0, D)
+        load_scales(wsk, Wk_scales, 0, D, ALL)
         load_w_codes(0, 1)
         load_w_codes(0, 3)
-        load_scales(wsq[1], Wq_scales, NB, NB)
-        load_scales(wsq[3], Wq_scales, 3 * NB, NB)
+        load_scales(wsq[1], Wq_scales, NB, NB, ALL)
+        load_scales(wsq[3], Wq_scales, 3 * NB, NB, ALL)
         for pt in range(4):
             load_table(nc.sync, pt, 1)
         load_w_codes(1, 1)
@@ -114,7 +136,7 @@ def tile_attention_pa_kernel(
         for pt in range(4):
             negate_table(pt, 0)
 
-        def bank(ab, proj, h, pp, b, u, half):
+        def bank(ab, i, proj, h, pp, b, u, half):
             n = h + 2 * half
             acc = psum.tile([P, NB], F32, name="acc")
             for g in range(PASSES):
@@ -133,50 +155,59 @@ def tile_attention_pa_kernel(
                 )
             table = th[(2 * pp + u, h)]
             if half == 0:
-                dst = ab[:, 2 * u : 2 * u + 6 : 5, :]
+                dst = ab[:, 2 * i : 2 * i + 2 * U + 2 : 2 * U + 1, :]
                 tab = table[:, 0:4:3, :]
             else:
-                dst = ab[:, 2 * u + 1 : 2 * u + 5 : 3, :]
+                dst = ab[:, 2 * i + 1 : 2 * i + 2 * U + 1 : 2 * U - 1, :]
                 tab = table[:, 1:3, :]
             nc.vector.tensor_tensor(
                 out=dst, in0=acc[:].unsqueeze(1).to_broadcast([P, 2, NB]), in1=tab, op=MULT
             )
 
-        def store(ab, proj, h, pp, b, u):
-            nc.scalar.dma_start(out=out_v[proj][b, 2 * pp + u, :, h:4:2, :], in_=ab[:, 2 * u : 2 * u + 2, :])
+        def add(eng, ab, lo, hi):
+            eng.tensor_tensor(out=ab[:, lo:hi, :], in0=ab[:, lo:hi, :], in1=ab[:, 2 * U + lo : 2 * U + hi, :], op=ADD)
 
-        units = []
+        blocks = []
         for proj, h in ((0, 0), (1, 0), (0, 1), (1, 1)):
             for pp in range(2):
                 for b in range(B):
-                    units.append((proj, h, pp, b))
-
-        for k, (proj, h, pp, b) in enumerate(units):
-            if k == 4:
-                for pt in range(4):
-                    negate_table(pt, 1)
-            ab = work.tile([P, 8, NB], F32, name="ab")
-            if k < len(units) - 2:
-                for half in range(2):
                     for u in range(2):
-                        bank(ab, proj, h, pp, b, u, half)
-                nc.gpsimd.tensor_tensor(out=ab[:, 0:4, :], in0=ab[:, 0:4, :], in1=ab[:, 4:8, :], op=ADD)
-                for u in range(2):
-                    store(ab, proj, h, pp, b, u)
-            else:
-                for u in range(2):
+                        blocks.append((proj, h, pp, b, u))
+
+        def store(eng, ab, s):
+            proj, h, pp, b, u = blocks[s]
+            i = s % U
+            eng.dma_start(out=out_v[proj][b, 2 * pp + u, :, h:4:2, :], in_=ab[:, 2 * i : 2 * i + 2, :])
+
+        first_v = len(blocks) - V_BLOCKS
+        ab_tiles = []
+        for j in range(len(blocks) // U):
+            ab = work.tile([P, 4 * U, NB], F32, name="ab")
+            ab_tiles.append(ab)
+            lo = 0
+            for size in add_sizes(j):
+                for i in range(lo, lo + size):
+                    s = U * j + i
+                    if s == 8:
+                        for pt in range(4):
+                            negate_table(pt, 1)
+                    proj, h, pp, b, u = blocks[s]
                     for half in range(2):
-                        bank(ab, proj, h, pp, b, u, half)
-                    if k == len(units) - 1 and u == 1:
-                        for j in (2, 3):
-                            nc.vector.tensor_tensor(
-                                out=ab[:, j, :], in0=ab[:, j, :], in1=ab[:, j + 4, :], op=ADD
-                            )
-                    else:
-                        nc.gpsimd.tensor_tensor(
-                            out=ab[:, 2 * u : 2 * u + 2, :],
-                            in0=ab[:, 2 * u : 2 * u + 2, :],
-                            in1=ab[:, 2 * u + 4 : 2 * u + 6, :],
-                            op=ADD,
-                        )
-                    store(ab, proj, h, pp, b, u)
+                        bank(ab, i, proj, h, pp, b, u, half)
+                if U * j + lo < first_v:
+                    add(nc.gpsimd, ab, 2 * lo, 2 * (lo + size))
+                    for i in range(lo, lo + size):
+                        store(nc.scalar, ab, U * j + i)
+                lo += size
+        for s in range(first_v, len(blocks) - 1):
+            i = s % U
+            add(nc.vector, ab_tiles[s // U], 2 * i, 2 * i + 2)
+            store(nc.scalar, ab_tiles[s // U], s)
+        s = len(blocks) - 1
+        proj, h, pp, b, u = blocks[s]
+        i = s % U
+        for blk, eng in ((0, nc.sync), (1, nc.scalar)):
+            add(nc.vector, ab_tiles[s // U], 2 * i + blk, 2 * i + blk + 1)
+            eng.dma_start(
+                out=out_v[proj][b, 2 * pp + u, :, h + 2 * blk, :], in_=ab_tiles[s // U][:, 2 * i + blk, :]
+            )

@@ -16,7 +16,7 @@ PASSES = D // 512
 NB = 512
 U = 4
 V_BLOCKS = 5
-WARM = 12
+WARM = 6
 
 FLOPS = 2 * B * S * D * 2 * D
 

@@ -53,14 +53,20 @@ def tile_attention_pa_kernel(
         xc = {}
         for b in range(B):
             for pp in range(2):
-                xc[(b, pp)] = keep.tile([P, PASSES, 512], U8, name="xc%d_%d" % (b, pp), align_bytes=64)
-        xs = [keep.tile([P, PASSES, S], U8, name="xs%d" % b, align_bytes=64) for b in range(B)]
+                raw = keep.tile([P, PASSES * 512 + 256], U8, name="xc%d_%d" % (b, pp), align_bytes=256)
+                r = 64 * ((2 * b + pp) % 4)
+                xc[(b, pp)] = raw[:, r : r + PASSES * 512].rearrange("p (g c) -> p g c", g=PASSES)
+        xs_raw = [keep.tile([P, PASSES * S + 256], U8, name="xs%d" % b, align_bytes=256) for b in range(B)]
+        xs = [
+            xs_raw[b][:, 64 * (b % 4) : 64 * (b % 4) + PASSES * S].rearrange("p (g c) -> p g c", g=PASSES)
+            for b in range(B)
+        ]
         wc = {}
         for proj in range(2):
             for n in range(4):
-                wc[(proj, n)] = keep.tile([P, PASSES, 2 * NB], U8, name="wc%d_%d" % (proj, n), align_bytes=64)
-        wsq = [keep.tile([P, PASSES, NB], U8, name="wsq%d" % n, align_bytes=64) for n in range(4)]
-        wsk = keep.tile([P, PASSES, D], U8, name="wsk", align_bytes=64)
+                wc[(proj, n)] = keep.tile([P, PASSES, 2 * NB], U8, name="wc%d_%d" % (proj, n), align_bytes=256)
+        wsq = [keep.tile([P, PASSES, NB], U8, name="wsq%d" % n, align_bytes=256) for n in range(4)]
+        wsk = keep.tile([P, PASSES, D], U8, name="wsk", align_bytes=256)
         th = {}
         for pt in range(4):
             for h in range(2):
@@ -82,7 +88,7 @@ def tile_attention_pa_kernel(
 
         def load_x_codes(b, pp):
             off = 2 * (S * b + 256 * pp)
-            nc.sync.dma_start(out=xc[(b, pp)][:].bitcast(I32), in_=x_v[:, :, off : off + 512].bitcast(I32))
+            nc.sync.dma_start(out=xc[(b, pp)].bitcast(I32), in_=x_v[:, :, off : off + 512].bitcast(I32))
 
         def load_w_codes(proj, n):
             nc.sync.dma_start(
@@ -92,7 +98,7 @@ def tile_attention_pa_kernel(
 
         ALL = (0, 1, 2, 3)
 
-        nc.gpsimd.memset(xs[0][:].bitcast(F32), 0.0)
+        nc.gpsimd.memset(xs_raw[0][:].bitcast(F32), 0.0)
         if WARM:
             zero = keep.tile([P, NB], BF16, name="zero")
             nc.gpsimd.memset(zero[:], 0.0)
@@ -101,9 +107,9 @@ def tile_attention_pa_kernel(
                 nc.tensor.matmul(out=warm[:], lhsT=zero[:, 0:P], rhs=zero[:], start=True, stop=True)
         load_table(nc.gpsimd, 0, 0)
         load_table(nc.gpsimd, 1, 0)
-        for plane in (wsq[0], wsq[2], xs[1]):
+        for plane in (wsq[0], wsq[2], xs_raw[1]):
             nc.vector.memset(plane[:].bitcast(I32), 0)
-        for plane in (xs[2], xs[3], xs[4], wsk, wsq[1], wsq[3]):
+        for plane in (xs_raw[2], xs_raw[3], xs_raw[4], wsk, wsq[1], wsq[3]):
             nc.gpsimd.memset(plane[:].bitcast(F32), 0.0)
 
         load_x_codes(0, 0)

@@ -1,6 +1,7 @@
 from contextlib import ExitStack
 
 import concourse.mybir as mybir
+from concourse.masks import make_identity
 
 F32 = mybir.dt.float32
 BF16 = mybir.dt.bfloat16
@@ -16,6 +17,7 @@ PASSES = D // 512
 NB = 512
 U = 4
 V_BLOCKS = 5
+PE_BLOCKS = 1
 WARM = 6
 
 FLOPS = 2 * B * S * D * 2 * D
@@ -111,6 +113,8 @@ def tile_attention_pa_kernel(
             nc.vector.memset(plane[:].bitcast(I32), 0)
         for plane in (xs_raw[2], xs_raw[3], xs_raw[4], wsk, wsq[1], wsq[3]):
             nc.gpsimd.memset(plane[:].bitcast(F32), 0.0)
+        ident = keep.tile([P, P], F32, name="ident")
+        make_identity(nc, ident[:])
 
         load_x_codes(0, 0)
         load_scales(xs[0], x_scales, 0, S, ALL)
@@ -203,12 +207,22 @@ def tile_attention_pa_kernel(
                 if U * j + lo < first_v:
                     add(nc.gpsimd, ab, 2 * lo, 2 * (lo + size))
                     for i in range(lo, lo + size):
-                        store(nc.scalar, ab, U * j + i)
+                        store(nc.sync if j >= 18 else nc.scalar, ab, U * j + i)
                 lo += size
-        for s in range(first_v, len(blocks) - 1):
+        for s in range(first_v, first_v + PE_BLOCKS):
+            proj, h, pp, b, u = blocks[s]
+            i = s % U
+            ab = ab_tiles[s // U]
+            for blk in range(2):
+                acc = psum.tile([P, NB], F32, name="acc")
+                nc.tensor.matmul(out=acc[:], lhsT=ident[:], rhs=ab[:, 2 * i + blk, :], start=True, stop=False)
+                nc.tensor.matmul(out=acc[:], lhsT=ident[:], rhs=ab[:, 2 * U + 2 * i + blk, :], start=False, stop=True)
+                nc.scalar.copy(out=ab[:, 2 * i + blk, :], in_=acc[:])
+                nc.scalar.dma_start(out=out_v[proj][b, 2 * pp + u, :, h + 2 * blk, :], in_=ab[:, 2 * i + blk, :])
+        for s in range(first_v + PE_BLOCKS, len(blocks) - 1):
             i = s % U
             add(nc.vector, ab_tiles[s // U], 2 * i, 2 * i + 2)
-            store(nc.scalar, ab_tiles[s // U], s)
+            store(nc.sync, ab_tiles[s // U], s)
         s = len(blocks) - 1
         proj, h, pp, b, u = blocks[s]
         i = s % U

@@ -101,6 +101,7 @@ def tile_attention_pa_kernel(
         ALL = (0, 1, 2, 3)
 
         nc.gpsimd.memset(xs_raw[0][:].bitcast(F32), 0.0)
+        nc.gpsimd.memset(wsq[0][:].bitcast(F32), 0.0)
         if WARM:
             zero = keep.tile([P, NB], BF16, name="zero")
             nc.gpsimd.memset(zero[:], 0.0)
@@ -109,7 +110,7 @@ def tile_attention_pa_kernel(
                 nc.tensor.matmul(out=warm[:], lhsT=zero[:, 0:P], rhs=zero[:], start=True, stop=True)
         load_table(nc.gpsimd, 0, 0)
         load_table(nc.gpsimd, 1, 0)
-        for plane in (wsq[0], wsq[2], xs_raw[1]):
+        for plane in (wsq[2], xs_raw[1]):
             nc.vector.memset(plane[:].bitcast(I32), 0)
         for plane in (xs_raw[2], xs_raw[3], xs_raw[4], wsk, wsq[1], wsq[3]):
             nc.gpsimd.memset(plane[:].bitcast(F32), 0.0)

@@ -18,7 +18,8 @@ NB = 512
 U = 4
 V_BLOCKS = 5
 PE_BLOCKS = 1
-WARM = 6
+WARM = 8
+BANK_ORDER = (0, 4, 1, 5, 2, 6, 3, 7)
 
 FLOPS = 2 * B * S * D * 2 * D
 
@@ -50,7 +51,7 @@ def tile_attention_pa_kernel(
         ctx.enter_context(tc.manual_schedule())
         keep = ctx.enter_context(tc.tile_pool(name="keep", bufs=1))
         work = ctx.enter_context(tc.tile_pool(name="work", bufs=3))
-        psum = ctx.enter_context(tc.psum_pool(name="psum", bufs=8))
+        psum = ctx.enter_context(tc.psum_pool(name="psum", bufs=1))
 
         xc = {}
         for b in range(B):
@@ -105,8 +106,8 @@ def tile_attention_pa_kernel(
         if WARM:
             zero = keep.tile([P, NB], BF16, name="zero")
             nc.gpsimd.memset(zero[:], 0.0)
-            warm = psum.tile([P, NB], F32, name="acc")
             for r in range(WARM):
+                warm = psum.tile([P, NB], F32, name="acc%d" % r)
                 nc.tensor.matmul(out=warm[:], lhsT=zero[:, 0:P], rhs=zero[:], start=True, stop=True)
         load_table(nc.gpsimd, 0, 0)
         load_table(nc.gpsimd, 1, 0)
@@ -147,9 +148,15 @@ def tile_attention_pa_kernel(
         for pt in range(4):
             negate_table(pt, 0)
 
+        filled = []
+
+        def next_bank():
+            filled.append(0)
+            return psum.tile([P, NB], F32, name="acc%d" % BANK_ORDER[(len(filled) - 1) % 8])
+
         def bank(ab, i, proj, h, pp, b, u, half):
             n = h + 2 * half
-            acc = psum.tile([P, NB], F32, name="acc")
+            acc = next_bank()
             for g in range(PASSES):
                 if proj == 0:
                     rs = wsq[n][:, g, :]
@@ -215,7 +222,7 @@ def tile_attention_pa_kernel(
             i = s % U
             ab = ab_tiles[s // U]
             for blk in range(2):
-                acc = psum.tile([P, NB], F32, name="acc")
+                acc = next_bank()
                 nc.tensor.matmul(out=acc[:], lhsT=ident[:], rhs=ab[:, 2 * i + blk, :], start=True, stop=False)
                 nc.tensor.matmul(out=acc[:], lhsT=ident[:], rhs=ab[:, 2 * U + 2 * i + blk, :], start=False, stop=True)
                 nc.scalar.copy(out=ab[:, 2 * i + blk, :], in_=acc[:])

@@ -19,7 +19,7 @@ U = 4
 V_BLOCKS = 5
 PE_BLOCKS = 1
 WARM = 8
-BANK_ORDER = (0, 4, 1, 5, 2, 6, 3, 7)
+BANK_ORDER = (0, 3, 6, 1, 4, 7, 2, 5)
 
 FLOPS = 2 * B * S * D * 2 * D
 

from contextlib import ExitStack

import concourse.mybir as mybir
from concourse.masks import make_identity

F32 = mybir.dt.float32
BF16 = mybir.dt.bfloat16
I32 = mybir.dt.int32
U8 = mybir.dt.uint8
FP4X4 = mybir.dt.float4_e2m1fn_x4
MULT = mybir.AluOpType.mult
ADD = mybir.AluOpType.add

B, S, D = 5, 512, 2048
P = 128
PASSES = D // 512
NB = 512
U = 4
V_BLOCKS = 5
PE_BLOCKS = 1
WARM = 8
BANK_ORDER = (0, 3, 6, 1, 4, 7, 2, 5)

FLOPS = 2 * B * S * D * 2 * D


def add_sizes(j):
    if j == 0:
        return (1, 1, 2)
    if j < 7:
        return (2, 2)
    if j < 18:
        return (4,)
    return (2, 1, 1)


def tile_attention_pa_kernel(
    tc, x_words, x_scales, cos, sin, Wq_words, Wq_scales, Wk_words, Wk_scales, out_0, out_1
):
    nc = tc.nc
    w_words = (Wq_words, Wk_words)
    outs = (out_0, out_1)

    cos_v = cos.rearrange("(t p) (n c) -> t p n c", p=P, c=NB)
    sin_v = sin.rearrange("(t p) (n c) -> t p n c", p=P, c=NB)
    out_v = [o.rearrange("b (t p) (n c) -> b t p n c", p=P, c=NB) for o in outs]
    x_v = x_words.rearrange("g p c -> p g c")
    w_v = [w.rearrange("g p c -> p g c") for w in w_words]

    with ExitStack() as ctx:
        ctx.enter_context(tc.manual_schedule())
        keep = ctx.enter_context(tc.tile_pool(name="keep", bufs=1))
        work = ctx.enter_context(tc.tile_pool(name="work", bufs=3))
        psum = ctx.enter_context(tc.psum_pool(name="psum", bufs=1))

        xc = {}
        for b in range(B):
            for pp in range(2):
                raw = keep.tile([P, PASSES * 512 + 256], U8, name="xc%d_%d" % (b, pp), align_bytes=256)
                r = 64 * ((2 * b + pp) % 4)
                xc[(b, pp)] = raw[:, r : r + PASSES * 512].rearrange("p (g c) -> p g c", g=PASSES)
        xs_raw = [keep.tile([P, PASSES * S + 256], U8, name="xs%d" % b, align_bytes=256) for b in range(B)]
        xs = [
            xs_raw[b][:, 64 * (b % 4) : 64 * (b % 4) + PASSES * S].rearrange("p (g c) -> p g c", g=PASSES)
            for b in range(B)
        ]
        wc = {}
        for proj in range(2):
            for n in range(4):
                wc[(proj, n)] = keep.tile([P, PASSES, 2 * NB], U8, name="wc%d_%d" % (proj, n), align_bytes=256)
        wsq = [keep.tile([P, PASSES, NB], U8, name="wsq%d" % n, align_bytes=256) for n in range(4)]
        wsk = keep.tile([P, PASSES, D], U8, name="wsk", align_bytes=256)
        th = {}
        for pt in range(4):
            for h in range(2):
                th[(pt, h)] = keep.tile([P, 4, NB], BF16, name="th%d_%d" % (pt, h))

        def load_table(eng, pt, h):
            eng.dma_start(out=th[(pt, h)][:, 0:2, :], in_=cos_v[pt, :, h:4:2, :])
            eng.dma_start(out=th[(pt, h)][:, 2:4, :], in_=sin_v[pt, :, h:4:2, :])

        def negate_table(pt, h):
            nc.scalar.mul(out=th[(pt, h)][:, 2, :], in_=th[(pt, h)][:, 2, :], mul=-1.0)

        def load_scales(plane, src, c0, ncols, quads):
            for q in quads:
                nc.sync.dma_start(
                    out=plane[32 * q : 32 * q + 4, :, :].bitcast(I32),
                    in_=src[:, 4 * q : 4 * q + 4, c0 : c0 + ncols].rearrange("g r n -> r g n").bitcast(I32),
                )

        def load_x_codes(b, pp):
            off = 2 * (S * b + 256 * pp)
            nc.sync.dma_start(out=xc[(b, pp)].bitcast(I32), in_=x_v[:, :, off : off + 512].bitcast(I32))

        def load_w_codes(proj, n):
            nc.sync.dma_start(
                out=wc[(proj, n)][:].bitcast(I32),
                in_=w_v[proj][:, :, 2 * NB * n : 2 * NB * (n + 1)].bitcast(I32),
            )

        ALL = (0, 1, 2, 3)

        nc.gpsimd.memset(xs_raw[0][:].bitcast(F32), 0.0)
        nc.gpsimd.memset(wsq[0][:].bitcast(F32), 0.0)
        if WARM:
            zero = keep.tile([P, NB], BF16, name="zero")
            nc.gpsimd.memset(zero[:], 0.0)
            for r in range(WARM):
                warm = psum.tile([P, NB], F32, name="acc%d" % r)
                nc.tensor.matmul(out=warm[:], lhsT=zero[:, 0:P], rhs=zero[:], start=True, stop=True)
        load_table(nc.gpsimd, 0, 0)
        load_table(nc.gpsimd, 1, 0)
        for plane in (wsq[2], xs_raw[1]):
            nc.vector.memset(plane[:].bitcast(I32), 0)
        for plane in (xs_raw[2], xs_raw[3], xs_raw[4], wsk, wsq[1], wsq[3]):
            nc.gpsimd.memset(plane[:].bitcast(F32), 0.0)
        ident = keep.tile([P, P], F32, name="ident")
        make_identity(nc, ident[:])

        load_x_codes(0, 0)
        load_scales(xs[0], x_scales, 0, S, ALL)
        load_scales(wsq[0], Wq_scales, 0, NB, (0, 1))
        load_w_codes(0, 0)
        load_scales(wsq[0], Wq_scales, 0, NB, (2, 3))
        load_w_codes(0, 2)
        load_scales(wsq[2], Wq_scales, 2 * NB, NB, ALL)
        for b in range(1, B):
            load_scales(xs[b], x_scales, S * b, S, ALL)
            load_x_codes(b, 0)
        load_x_codes(0, 1)
        load_table(nc.sync, 2, 0)
        load_table(nc.sync, 3, 0)
        for b in range(1, B):
            load_x_codes(b, 1)
        load_w_codes(1, 0)
        load_w_codes(1, 2)
        load_scales(wsk, Wk_scales, 0, D, ALL)
        load_w_codes(0, 1)
        load_w_codes(0, 3)
        load_scales(wsq[1], Wq_scales, NB, NB, ALL)
        load_scales(wsq[3], Wq_scales, 3 * NB, NB, ALL)
        for pt in range(4):
            load_table(nc.sync, pt, 1)
        load_w_codes(1, 1)
        load_w_codes(1, 3)

        for pt in range(4):
            negate_table(pt, 0)

        filled = []

        def next_bank():
            filled.append(0)
            return psum.tile([P, NB], F32, name="acc%d" % BANK_ORDER[(len(filled) - 1) % 8])

        def bank(ab, i, proj, h, pp, b, u, half):
            n = h + 2 * half
            acc = next_bank()
            for g in range(PASSES):
                if proj == 0:
                    rs = wsq[n][:, g, :]
                else:
                    rs = wsk[:, g, NB * n : NB * (n + 1)]
                nc.tensor.matmul_mx(
                    out=acc[:],
                    lhsT=xc[(b, pp)][:, g, 256 * u : 256 * (u + 1)].bitcast(FP4X4),
                    lhsT_scale=xs[b][:, g, 256 * pp + P * u : 256 * pp + P * (u + 1)],
                    rhs=wc[(proj, n)][:, g, :].bitcast(FP4X4),
                    rhs_scale=rs,
                    start=(g == 0),
                    stop=(g == PASSES - 1),
                )
            table = th[(2 * pp + u, h)]
            if half == 0:
                dst = ab[:, 2 * i : 2 * i + 2 * U + 2 : 2 * U + 1, :]
                tab = table[:, 0:4:3, :]
            else:
                dst = ab[:, 2 * i + 1 : 2 * i + 2 * U + 1 : 2 * U - 1, :]
                tab = table[:, 1:3, :]
            nc.vector.tensor_tensor(
                out=dst, in0=acc[:].unsqueeze(1).to_broadcast([P, 2, NB]), in1=tab, op=MULT
            )

        def add(eng, ab, lo, hi):
            eng.tensor_tensor(out=ab[:, lo:hi, :], in0=ab[:, lo:hi, :], in1=ab[:, 2 * U + lo : 2 * U + hi, :], op=ADD)

        blocks = []
        for proj, h in ((0, 0), (1, 0), (0, 1), (1, 1)):
            for pp in range(2):
                for b in range(B):
                    for u in range(2):
                        blocks.append((proj, h, pp, b, u))

        def store(eng, ab, s):
            proj, h, pp, b, u = blocks[s]
            i = s % U
            eng.dma_start(out=out_v[proj][b, 2 * pp + u, :, h:4:2, :], in_=ab[:, 2 * i : 2 * i + 2, :])

        first_v = len(blocks) - V_BLOCKS
        ab_tiles = []
        for j in range(len(blocks) // U):
            ab = work.tile([P, 4 * U, NB], F32, name="ab")
            ab_tiles.append(ab)
            lo = 0
            for size in add_sizes(j):
                for i in range(lo, lo + size):
                    s = U * j + i
                    if s == 8:
                        for pt in range(4):
                            negate_table(pt, 1)
                    proj, h, pp, b, u = blocks[s]
                    for half in range(2):
                        bank(ab, i, proj, h, pp, b, u, half)
                if U * j + lo < first_v:
                    add(nc.gpsimd, ab, 2 * lo, 2 * (lo + size))
                    for i in range(lo, lo + size):
                        store(nc.sync if j >= 18 else nc.scalar, ab, U * j + i)
                lo += size
        for s in range(first_v, first_v + PE_BLOCKS):
            proj, h, pp, b, u = blocks[s]
            i = s % U
            ab = ab_tiles[s // U]
            for blk in range(2):
                acc = next_bank()
                nc.tensor.matmul(out=acc[:], lhsT=ident[:], rhs=ab[:, 2 * i + blk, :], start=True, stop=False)
                nc.tensor.matmul(out=acc[:], lhsT=ident[:], rhs=ab[:, 2 * U + 2 * i + blk, :], start=False, stop=True)
                nc.scalar.copy(out=ab[:, 2 * i + blk, :], in_=acc[:])
                nc.scalar.dma_start(out=out_v[proj][b, 2 * pp + u, :, h + 2 * blk, :], in_=ab[:, 2 * i + blk, :])
        for s in range(first_v + PE_BLOCKS, len(blocks) - 1):
            i = s % U
            add(nc.vector, ab_tiles[s // U], 2 * i, 2 * i + 2)
            store(nc.sync, ab_tiles[s // U], s)
        s = len(blocks) - 1
        proj, h, pp, b, u = blocks[s]
        i = s % U
        for blk, eng in ((0, nc.sync), (1, nc.scalar)):
            add(nc.vector, ab_tiles[s // U], 2 * i + blk, 2 * i + blk + 1)
            eng.dma_start(
                out=out_v[proj][b, 2 * pp + u, :, h + 2 * blk, :], in_=ab_tiles[s // U][:, 2 * i + blk, :]
            )
